import numpy as np
import ml_dtypes


def mxq(x, axis, fmt="e4m3"):
    dtype, down = {"e4m3": (ml_dtypes.float8_e4m3fn, 7), "e5m2": (ml_dtypes.float8_e5m2, 14)}[fmt]
    v = np.moveaxis(np.asarray(x, np.float32).astype(ml_dtypes.bfloat16).astype(np.float64), axis, -1)
    blocks = v.reshape(v.shape[:-1] + (-1, 32))
    amax = np.abs(blocks).max(-1, keepdims=True)
    byte = np.maximum(np.where(amax > 0, np.frexp(amax)[1] - 1 + 127, 0) - down, 1)
    scale = np.exp2(byte - 127.0)
    codes = (blocks / scale).astype(np.float32).astype(dtype).astype(np.float64)
    return np.moveaxis((codes * scale).reshape(v.shape), -1, axis)


BF16 = ml_dtypes.bfloat16


def bf(x):
    return np.asarray(x, np.float32).astype(BF16)


def f64(x):
    return np.asarray(x).astype(np.float64)


N, M, H, D, R = 4096, 128, 8, 512, 4


def draw(rows, u):
    z = np.random.standard_normal((H, rows, R)) * 1.4 / np.sqrt(R)
    g = np.exp(0.5 * np.random.standard_normal((rows, H, 1)))
    v = (z @ u).transpose(1, 0, 2) + np.random.standard_normal((rows, H, D))
    return bf((v * g).reshape(rows, H * D))


def setup_inputs():
    u = np.random.standard_normal((H, R, D))
    return {"batch_s": draw(N, u), "batch_ro": draw(M, u)}


def reference(batch_s, batch_ro):
    s = f64(batch_s).reshape(N, H, D)
    ro = f64(batch_ro).reshape(M, H, D)
    s = s / np.linalg.norm(s, axis=-1, keepdims=True)
    ro = ro / np.linalg.norm(ro, axis=-1, keepdims=True)
    sq = mxq(s, 2, "e4m3")
    roq = mxq(ro, 2, "e4m3")
    dist = sq.transpose(1, 0, 2) @ roq.transpose(1, 2, 0)
    return dist.max(axis=0)

@@ -1,0 +1,210 @@
+from contextlib import ExitStack
+
+import concourse.mybir as mybir
+from concourse.masks import make_identity
+
+F32 = mybir.dt.float32
+BF16 = mybir.dt.bfloat16
+U32 = mybir.dt.uint32
+U8 = mybir.dt.uint8
+FP8X4 = mybir.dt.float8_e4m3fn_x4
+ACT = mybir.ActivationFunctionType
+ALU = mybir.AluOpType
+AXIS = mybir.AxisListType
+
+P = 128
+HEADS = 8
+D_HEAD = 512
+ROW = HEADS * D_HEAD
+N_ROWS = 4096
+S_TILES = N_ROWS // P
+ITEMS = 1 + S_TILES
+WORDS_HEAD = D_HEAD // 2
+BANK_WORDS = 512
+HEADS_BANK = BANK_WORDS // WORDS_HEAD
+T_BANKS = HEADS // HEADS_BANK
+HEADS_ACC = BANK_WORDS // P
+ACC_BANKS = HEADS // HEADS_ACC
+STORE_TILES = 4
+LOADS_AHEAD = 2
+
+FLOPS = 2 * N_ROWS * P * ROW
+
+
+def tile_multiheaddistance_t_kernel(tc, batch_s, batch_ro, out):
+    nc = tc.nc
+
+    s_tiles = batch_s.rearrange("(p t) d -> p t d", t=S_TILES)
+    out_tiles = out.rearrange("(p t) m -> p t m", t=S_TILES)
+
+    with ExitStack() as ctx:
+        keep = ctx.enter_context(tc.tile_pool(name="keep", bufs=1))
+        raw_pool = ctx.enter_context(tc.tile_pool(name="raw", bufs=LOADS_AHEAD + 2))
+        small = ctx.enter_context(tc.tile_pool(name="small", bufs=3))
+        unit_pool = ctx.enter_context(tc.tile_pool(name="unit", bufs=2))
+        grouped_pool = ctx.enter_context(tc.tile_pool(name="grouped", bufs=2))
+        mx_pool = ctx.enter_context(tc.tile_pool(name="mx", bufs=2))
+        part_pool = ctx.enter_context(tc.tile_pool(name="part", bufs=2))
+        t_psum = ctx.enter_context(tc.psum_pool(name="t_psum", bufs=T_BANKS))
+        acc_psum = ctx.enter_context(tc.psum_pool(name="acc_psum", bufs=2 * ACC_BANKS))
+
+        identity = keep.tile([P, P], F32)
+        make_identity(nc, identity[:])
+
+        one = keep.tile([P, 1], F32)
+        nc.vector.memset(one[:], 1.0)
+        warm = keep.tile([P, 1], F32)
+        nc.scalar.activation(out=warm[:], in_=one[:], func=ACT.Sqrt)
+
+        squared = keep.tile([P, ROW], BF16)
+
+        ro_codes = keep.tile([P, HEADS * P], U32, align_bytes=64)
+        ro_scales = keep.tile([P, HEADS * P], U8, align_bytes=64)
+        result = keep.tile([P, S_TILES, P], F32)
+
+        raw_of = {}
+        sumsq_of = {}
+        norm_of = {}
+        inv_of = {}
+        unit_of = {}
+        banks_of = {}
+        grouped_of = {}
+        codes_of = {}
+        scales_of = {}
+        acc_of = {}
+        part_of = {}
+
+        def head_cols(h):
+            return slice(h * D_HEAD, (h + 1) * D_HEAD)
+
+        def head_rows(h):
+            return slice(h * P, (h + 1) * P)
+
+        def load(j):
+            raw = raw_pool.tile([P, ROW], BF16)
+            nc.sync.dma_start(out=raw[:], in_=batch_ro if j == 0 else s_tiles[:, j - 1, :])
+            raw_of[j] = raw
+
+        def squares(j):
+            sumsq = small.tile([P, HEADS], F32)
+            for h in range(HEADS):
+                nc.scalar.activation(
+                    out=squared[:, head_cols(h)],
+                    in_=raw_of[j][:, head_cols(h)],
+                    func=ACT.Square,
+                    accum_out=sumsq[:, h : h + 1],
+                )
+            sumsq_of[j] = sumsq
+
+        def norms(j):
+            norm = small.tile([P, HEADS], F32)
+            nc.scalar.activation(out=norm[:], in_=sumsq_of[j][:], func=ACT.Sqrt)
+            norm_of[j] = norm
+
+        def inverse(j):
+            inv = small.tile([P, HEADS], F32)
+            nc.vector.reciprocal(out=inv[:], in_=norm_of[j][:])
+            inv_of[j] = inv
+
+        def normalise(j):
+            unit = unit_pool.tile([P, ROW], BF16)
+            for h in range(HEADS):
+                nc.vector.tensor_scalar_mul(
+                    out=unit[:, head_cols(h)],
+                    in0=raw_of[j][:, head_cols(h)],
+                    scalar1=inv_of[j][:, h : h + 1],
+                )
+            unit_of[j] = unit
+
+        def transposes(j):
+            words = unit_of[j][:].bitcast(F32)
+            banks = []
+            for b in range(T_BANKS):
+                bank = t_psum.tile([P, 2 * HEADS_BANK, P], F32)
+                for plane in range(2 * HEADS_BANK):
+                    first = (b * 2 * HEADS_BANK + plane) * P
+                    nc.tensor.transpose(bank[:, plane, :], words[:, first : first + P], identity[:])
+                banks.append(bank)
+            banks_of[j] = banks
+
+        def regroup(j):
+            grouped = grouped_pool.tile([P, ROW], BF16, align_bytes=64)
+            pairs = grouped[:].bitcast(F32).rearrange("p (h r u) -> p h r u", h=HEADS, u=2)
+            for b in range(T_BANKS):
+                planes = banks_of[j][b][:].rearrange("p (h u) r -> p h r u", u=2)
+                target = pairs[:, b * HEADS_BANK : (b + 1) * HEADS_BANK]
+                if b == 0:
+                    nc.scalar.copy(out=target, in_=planes)
+                else:
+                    nc.vector.tensor_copy(out=target, in_=planes)
+            grouped_of[j] = grouped
+
+        def quantise(j):
+            if j == 0:
+                codes, scales = ro_codes, ro_scales
+            else:
+                codes = mx_pool.tile([P, HEADS * P], U32, align_bytes=64)
+                scales = mx_pool.tile([P, HEADS * P], U8, align_bytes=64)
+            nc.vector.quantize_mx(
+                out=codes[:].bitcast(FP8X4), scales=scales[:], in_=grouped_of[j][:]
+            )
+            codes_of[j] = codes
+            scales_of[j] = scales
+
+        def matmuls(j):
+            accs = []
+            for a in range(ACC_BANKS):
+                acc = acc_psum.tile([P, HEADS_ACC, P], F32)
+                for i in range(HEADS_ACC):
+                    rows = head_rows(a * HEADS_ACC + i)
+                    nc.tensor.matmul_mx(
+                        out=acc[:, i, :],
+                        lhsT=codes_of[j][:, rows].bitcast(FP8X4),
+                        lhsT_scale=scales_of[j][:, rows],
+                        rhs=ro_codes[:, rows].bitcast(FP8X4),
+                        rhs_scale=ro_scales[:, rows],
+                        start=True,
+                        stop=True,
+                    )
+                accs.append(acc)
+            acc_of[j] = accs
+
+        def head_max(j):
+            t = j - 1
+            place = t % STORE_TILES
+            if place == 0:
+                part = part_pool.tile([P, STORE_TILES, ACC_BANKS, P], F32)
+                part_of[t // STORE_TILES] = part
+            part = part_of[t // STORE_TILES]
+            for a in range(ACC_BANKS):
+                nc.vector.tensor_reduce(
+                    out=part[:, place, a, :],
+                    in_=acc_of[j][a][:].rearrange("p h m -> p m h"),
+                    axis=AXIS.X,
+                    op=ALU.max,
+                )
+            if place == STORE_TILES - 1:
+                done = slice(t - place, t + 1)
+                nc.vector.tensor_max(
+                    out=result[:, done, :], in0=part[:, :, 0, :], in1=part[:, :, 1, :]
+                )
+                nc.sync.dma_start(out=out_tiles[:, done, :], in_=result[:, done, :])
+
+        def staged(stage, j, first=0):
+            if first <= j < ITEMS:
+                stage(j)
+
+        ctx.enter_context(tc.manual_schedule())
+        for j in range(LOADS_AHEAD):
+            load(j)
+        for k in range(ITEMS + 3):
+            staged(load, k + LOADS_AHEAD)
+            staged(quantise, k - 3)
+            staged(matmuls, k - 3, first=1)
+            staged(regroup, k - 2)
+            staged(norms, k - 1)
+            staged(inverse, k - 1)
+            staged(head_max, k - 3, first=1)
+            staged(normalise, k - 1)
+            staged(transposes, k - 1)
+            staged(squares, k)

@@ -26,6 +26,7 @@ T_BANKS = HEADS // HEADS_BANK
 HEADS_ACC = BANK_WORDS // P
 ACC_BANKS = HEADS // HEADS_ACC
 STORE_TILES = 4
+VECTOR_UNITS = 3
 LOADS_AHEAD = 2
 
 FLOPS = 2 * N_ROWS * P * ROW
@@ -45,8 +46,8 @@ def tile_multiheaddistance_t_kernel(tc, batch_s, batch_ro, out):
         grouped_pool = ctx.enter_context(tc.tile_pool(name="grouped", bufs=2))
         mx_pool = ctx.enter_context(tc.tile_pool(name="mx", bufs=2))
         part_pool = ctx.enter_context(tc.tile_pool(name="part", bufs=2))
-        t_psum = ctx.enter_context(tc.psum_pool(name="t_psum", bufs=T_BANKS))
-        acc_psum = ctx.enter_context(tc.psum_pool(name="acc_psum", bufs=2 * ACC_BANKS))
+        t_psum = ctx.enter_context(tc.psum_pool(name="t_psum", bufs=T_BANKS + 2))
+        acc_psum = ctx.enter_context(tc.psum_pool(name="acc_psum", bufs=ACC_BANKS))
 
         identity = keep.tile([P, P], F32)
         make_identity(nc, identity[:])
@@ -54,7 +55,7 @@ def tile_multiheaddistance_t_kernel(tc, batch_s, batch_ro, out):
         one = keep.tile([P, 1], F32)
         nc.vector.memset(one[:], 1.0)
         warm = keep.tile([P, 1], F32)
-        nc.scalar.activation(out=warm[:], in_=one[:], func=ACT.Sqrt)
+        nc.scalar.activation(out=warm[:], in_=one[:], func=ACT.Abs_reciprocal_sqrt)
 
         squared = keep.tile([P, ROW], BF16)
 
@@ -64,7 +65,6 @@ def tile_multiheaddistance_t_kernel(tc, batch_s, batch_ro, out):
 
         raw_of = {}
         sumsq_of = {}
-        norm_of = {}
         inv_of = {}
         unit_of = {}
         banks_of = {}
@@ -85,35 +85,41 @@ def tile_multiheaddistance_t_kernel(tc, batch_s, batch_ro, out):
             nc.sync.dma_start(out=raw[:], in_=batch_ro if j == 0 else s_tiles[:, j - 1, :])
             raw_of[j] = raw
 
-        def squares(j):
-            sumsq = small.tile([P, HEADS], F32)
-            for h in range(HEADS):
+        def squares(j, heads):
+            if 0 in heads:
+                sumsq = small.tile([P, HEADS], F32)
+                sumsq_of[j] = sumsq
+            for h in heads:
                 nc.scalar.activation(
                     out=squared[:, head_cols(h)],
                     in_=raw_of[j][:, head_cols(h)],
                     func=ACT.Square,
-                    accum_out=sumsq[:, h : h + 1],
+                    accum_out=sumsq_of[j][:, h : h + 1],
                 )
-            sumsq_of[j] = sumsq
-
-        def norms(j):
-            norm = small.tile([P, HEADS], F32)
-            nc.scalar.activation(out=norm[:], in_=sumsq_of[j][:], func=ACT.Sqrt)
-            norm_of[j] = norm
 
         def inverse(j):
             inv = small.tile([P, HEADS], F32)
-            nc.vector.reciprocal(out=inv[:], in_=norm_of[j][:])
+            nc.scalar.activation(out=inv[:], in_=sumsq_of[j][:], func=ACT.Abs_reciprocal_sqrt)
             inv_of[j] = inv
 
         def normalise(j):
             unit = unit_pool.tile([P, ROW], BF16)
             for h in range(HEADS):
-                nc.vector.tensor_scalar_mul(
-                    out=unit[:, head_cols(h)],
-                    in0=raw_of[j][:, head_cols(h)],
-                    scalar1=inv_of[j][:, h : h + 1],
-                )
+                if h < VECTOR_UNITS:
+                    nc.vector.tensor_scalar_mul(
+                        out=unit[:, head_cols(h)],
+                        in0=raw_of[j][:, head_cols(h)],
+                        scalar1=inv_of[j][:, h : h + 1],
+                    )
+                else:
+                    nc.gpsimd.tensor_scalar(
+                        out=unit[:, head_cols(h)],
+                        in0=raw_of[j][:, head_cols(h)],
+                        scalar1=inv_of[j][:, h : h + 1],
+                        scalar2=0.0,
+                        op0=ALU.mult,
+                        op1=ALU.add,
+                    )
             unit_of[j] = unit
 
         def transposes(j):
@@ -133,7 +139,7 @@ def tile_multiheaddistance_t_kernel(tc, batch_s, batch_ro, out):
             for b in range(T_BANKS):
                 planes = banks_of[j][b][:].rearrange("p (h u) r -> p h r u", u=2)
                 target = pairs[:, b * HEADS_BANK : (b + 1) * HEADS_BANK]
-                if b == 0:
+                if b == 0 and j % 2 == 0:
                     nc.scalar.copy(out=target, in_=planes)
                 else:
                     nc.vector.tensor_copy(out=target, in_=planes)
@@ -190,9 +196,9 @@ def tile_multiheaddistance_t_kernel(tc, batch_s, batch_ro, out):
                 )
                 nc.sync.dma_start(out=out_tiles[:, done, :], in_=result[:, done, :])
 
-        def staged(stage, j, first=0):
+        def staged(stage, j, *rest, first=0):
             if first <= j < ITEMS:
-                stage(j)
+                stage(j, *rest)
 
         ctx.enter_context(tc.manual_schedule())
         for j in range(LOADS_AHEAD):
@@ -201,10 +207,10 @@ def tile_multiheaddistance_t_kernel(tc, batch_s, batch_ro, out):
             staged(load, k + LOADS_AHEAD)
             staged(quantise, k - 3)
             staged(matmuls, k - 3, first=1)
-            staged(regroup, k - 2)
-            staged(norms, k - 1)
+            staged(squares, k, range(1))
             staged(inverse, k - 1)
-            staged(head_max, k - 3, first=1)
             staged(normalise, k - 1)
+            staged(regroup, k - 2)
             staged(transposes, k - 1)
-            staged(squares, k)
+            staged(head_max, k - 3, first=1)
+            staged(squares, k, range(1, HEADS))

@@ -66,6 +66,7 @@ def tile_multiheaddistance_t_kernel(tc, batch_s, batch_ro, out):
         raw_of = {}
         sumsq_of = {}
         inv_of = {}
+        gate_of = {}
         unit_of = {}
         banks_of = {}
         grouped_of = {}
@@ -102,25 +103,31 @@ def tile_multiheaddistance_t_kernel(tc, batch_s, batch_ro, out):
             nc.scalar.activation(out=inv[:], in_=sumsq_of[j][:], func=ACT.Abs_reciprocal_sqrt)
             inv_of[j] = inv
 
-        def normalise(j):
+        def release(j):
+            gate = small.tile([P, HEADS], F32)
+            nc.vector.tensor_copy(out=gate[:], in_=inv_of[j][:])
+            gate_of[j] = gate
+
+        def vector_units(j):
             unit = unit_pool.tile([P, ROW], BF16)
-            for h in range(HEADS):
-                if h < VECTOR_UNITS:
-                    nc.vector.tensor_scalar_mul(
-                        out=unit[:, head_cols(h)],
-                        in0=raw_of[j][:, head_cols(h)],
-                        scalar1=inv_of[j][:, h : h + 1],
-                    )
-                else:
-                    nc.gpsimd.tensor_scalar(
-                        out=unit[:, head_cols(h)],
-                        in0=raw_of[j][:, head_cols(h)],
-                        scalar1=inv_of[j][:, h : h + 1],
-                        scalar2=0.0,
-                        op0=ALU.mult,
-                        op1=ALU.add,
-                    )
+            for h in range(VECTOR_UNITS):
+                nc.vector.tensor_scalar_mul(
+                    out=unit[:, head_cols(h)],
+                    in0=raw_of[j][:, head_cols(h)],
+                    scalar1=inv_of[j][:, h : h + 1],
+                )
             unit_of[j] = unit
+
+        def gpsimd_units(j):
+            for h in range(VECTOR_UNITS, HEADS):
+                nc.gpsimd.tensor_scalar(
+                    out=unit_of[j][:, head_cols(h)],
+                    in0=raw_of[j][:, head_cols(h)],
+                    scalar1=gate_of[j][:, h : h + 1],
+                    scalar2=0.0,
+                    op0=ALU.mult,
+                    op1=ALU.add,
+                )
 
         def transposes(j):
             words = unit_of[j][:].bitcast(F32)
@@ -189,6 +196,11 @@ def tile_multiheaddistance_t_kernel(tc, batch_s, batch_ro, out):
                     axis=AXIS.X,
                     op=ALU.max,
                 )
+
+        def join(j):
+            t = j - 1
+            place = t % STORE_TILES
+            part = part_of[t // STORE_TILES]
             if place == STORE_TILES - 1:
                 done = slice(t - place, t + 1)
                 nc.vector.tensor_max(
@@ -203,13 +215,16 @@ def tile_multiheaddistance_t_kernel(tc, batch_s, batch_ro, out):
         ctx.enter_context(tc.manual_schedule())
         for j in range(LOADS_AHEAD):
             load(j)
-        for k in range(ITEMS + 3):
+        for k in range(ITEMS + 4):
             staged(load, k + LOADS_AHEAD)
             staged(quantise, k - 3)
             staged(matmuls, k - 3, first=1)
             staged(squares, k, range(1))
             staged(inverse, k - 1)
-            staged(normalise, k - 1)
+            staged(vector_units, k - 1)
+            staged(join, k - 4, first=1)
+            staged(release, k - 1)
+            staged(gpsimd_units, k - 1)
             staged(regroup, k - 2)
             staged(transposes, k - 1)
             staged(head_max, k - 3, first=1)

@@ -26,7 +26,7 @@ T_BANKS = HEADS // HEADS_BANK
 HEADS_ACC = BANK_WORDS // P
 ACC_BANKS = HEADS // HEADS_ACC
 STORE_TILES = 4
-VECTOR_UNITS = 3
+VECTOR_UNITS = 5
 LOADS_AHEAD = 2
 
 FLOPS = 2 * N_ROWS * P * ROW

@@ -27,6 +27,8 @@ HEADS_ACC = BANK_WORDS // P
 ACC_BANKS = HEADS // HEADS_ACC
 STORE_TILES = 4
 VECTOR_UNITS = 5
+VECTOR_SQUARES = {0: (2, 4, 6), 1: (3, 6), 2: (5,)}
+LOAD_PIECES = 4
 LOADS_AHEAD = 2
 
 FLOPS = 2 * N_ROWS * P * ROW
@@ -83,7 +85,11 @@ def tile_multiheaddistance_t_kernel(tc, batch_s, batch_ro, out):
 
         def load(j):
             raw = raw_pool.tile([P, ROW], BF16)
-            nc.sync.dma_start(out=raw[:], in_=batch_ro if j == 0 else s_tiles[:, j - 1, :])
+            rows = batch_ro if j == 0 else s_tiles[:, j - 1, :]
+            width = ROW // LOAD_PIECES if j < LOADS_AHEAD else ROW
+            for first in range(0, ROW, width):
+                cols = slice(first, first + width)
+                nc.sync.dma_start(out=raw[:, cols], in_=rows[:, cols])
             raw_of[j] = raw
 
         def squares(j, heads):
@@ -91,12 +97,24 @@ def tile_multiheaddistance_t_kernel(tc, batch_s, batch_ro, out):
                 sumsq = small.tile([P, HEADS], F32)
                 sumsq_of[j] = sumsq
             for h in heads:
-                nc.scalar.activation(
-                    out=squared[:, head_cols(h)],
-                    in_=raw_of[j][:, head_cols(h)],
-                    func=ACT.Square,
-                    accum_out=sumsq_of[j][:, h : h + 1],
-                )
+                values = raw_of[j][:, head_cols(h)]
+                if h in VECTOR_SQUARES.get(j, ()):
+                    nc.vector.scalar_tensor_tensor(
+                        out=squared[:, head_cols(h)],
+                        in0=values,
+                        scalar=1.0,
+                        in1=values,
+                        op0=ALU.mult,
+                        op1=ALU.mult,
+                        accum_out=sumsq_of[j][:, h : h + 1],
+                    )
+                else:
+                    nc.scalar.activation(
+                        out=squared[:, head_cols(h)],
+                        in_=values,
+                        func=ACT.Square,
+                        accum_out=sumsq_of[j][:, h : h + 1],
+                    )
 
         def inverse(j):
             inv = small.tile([P, HEADS], F32)
@@ -108,9 +126,12 @@ def tile_multiheaddistance_t_kernel(tc, batch_s, batch_ro, out):
             nc.vector.tensor_copy(out=gate[:], in_=inv_of[j][:])
             gate_of[j] = gate
 
+        def vector_share(j):
+            return HEADS if j == ITEMS - 1 else VECTOR_UNITS
+
         def vector_units(j):
             unit = unit_pool.tile([P, ROW], BF16)
-            for h in range(VECTOR_UNITS):
+            for h in range(vector_share(j)):
                 nc.vector.tensor_scalar_mul(
                     out=unit[:, head_cols(h)],
                     in0=raw_of[j][:, head_cols(h)],
@@ -119,7 +140,7 @@ def tile_multiheaddistance_t_kernel(tc, batch_s, batch_ro, out):
             unit_of[j] = unit
 
         def gpsimd_units(j):
-            for h in range(VECTOR_UNITS, HEADS):
+            for h in range(vector_share(j), HEADS):
                 nc.gpsimd.tensor_scalar(
                     out=unit_of[j][:, head_cols(h)],
                     in0=raw_of[j][:, head_cols(h)],
@@ -143,10 +164,11 @@ def tile_multiheaddistance_t_kernel(tc, batch_s, batch_ro, out):
         def regroup(j):
             grouped = grouped_pool.tile([P, ROW], BF16, align_bytes=64)
             pairs = grouped[:].bitcast(F32).rearrange("p (h r u) -> p h r u", h=HEADS, u=2)
+            scalar_banks = T_BANKS if j >= ITEMS - 2 else int(j % 4 != 3)
             for b in range(T_BANKS):
                 planes = banks_of[j][b][:].rearrange("p (h u) r -> p h r u", u=2)
                 target = pairs[:, b * HEADS_BANK : (b + 1) * HEADS_BANK]
-                if b == 0 and j % 2 == 0:
+                if b < scalar_banks:
                     nc.scalar.copy(out=target, in_=planes)
                 else:
                     nc.vector.tensor_copy(out=target, in_=planes)

@@ -18,16 +18,17 @@ D_HEAD = 512
 ROW = HEADS * D_HEAD
 N_ROWS = 4096
 S_TILES = N_ROWS // P
+LAST = S_TILES
 ITEMS = 1 + S_TILES
 WORDS_HEAD = D_HEAD // 2
 BANK_WORDS = 512
 HEADS_BANK = BANK_WORDS // WORDS_HEAD
 T_BANKS = HEADS // HEADS_BANK
-HEADS_ACC = BANK_WORDS // P
-ACC_BANKS = HEADS // HEADS_ACC
+RO_ACC = BANK_WORDS // HEADS
+ACC_BANKS = P // RO_ACC
 STORE_TILES = 4
 VECTOR_UNITS = 5
-VECTOR_SQUARES = {0: (2, 4, 6), 1: (3, 6), 2: (5,)}
+HEAD_SQUARES = (4, 5, 6, 7)
 LOAD_PIECES = 4
 LOADS_AHEAD = 2
 
@@ -47,7 +48,6 @@ def tile_multiheaddistance_t_kernel(tc, batch_s, batch_ro, out):
         unit_pool = ctx.enter_context(tc.tile_pool(name="unit", bufs=2))
         grouped_pool = ctx.enter_context(tc.tile_pool(name="grouped", bufs=2))
         mx_pool = ctx.enter_context(tc.tile_pool(name="mx", bufs=2))
-        part_pool = ctx.enter_context(tc.tile_pool(name="part", bufs=2))
         t_psum = ctx.enter_context(tc.psum_pool(name="t_psum", bufs=T_BANKS + 2))
         acc_psum = ctx.enter_context(tc.psum_pool(name="acc_psum", bufs=ACC_BANKS))
 
@@ -75,7 +75,6 @@ def tile_multiheaddistance_t_kernel(tc, batch_s, batch_ro, out):
         codes_of = {}
         scales_of = {}
         acc_of = {}
-        part_of = {}
 
         def head_cols(h):
             return slice(h * D_HEAD, (h + 1) * D_HEAD)
@@ -87,34 +86,54 @@ def tile_multiheaddistance_t_kernel(tc, batch_s, batch_ro, out):
             raw = raw_pool.tile([P, ROW], BF16)
             rows = batch_ro if j == 0 else s_tiles[:, j - 1, :]
             width = ROW // LOAD_PIECES if j < LOADS_AHEAD else ROW
-            for first in range(0, ROW, width):
+            for first in sorted(range(0, ROW, width), key=lambda col: col % (ROW // 2)):
                 cols = slice(first, first + width)
                 nc.sync.dma_start(out=raw[:, cols], in_=rows[:, cols])
             raw_of[j] = raw
+
+        def scalar_heads(j):
+            return HEAD_SQUARES[j] if j < len(HEAD_SQUARES) else HEADS
 
         def squares(j, heads):
             if 0 in heads:
                 sumsq = small.tile([P, HEADS], F32)
                 sumsq_of[j] = sumsq
             for h in heads:
-                values = raw_of[j][:, head_cols(h)]
-                if h in VECTOR_SQUARES.get(j, ()):
-                    nc.vector.scalar_tensor_tensor(
-                        out=squared[:, head_cols(h)],
-                        in0=values,
-                        scalar=1.0,
-                        in1=values,
-                        op0=ALU.mult,
-                        op1=ALU.mult,
-                        accum_out=sumsq_of[j][:, h : h + 1],
-                    )
-                else:
-                    nc.scalar.activation(
-                        out=squared[:, head_cols(h)],
-                        in_=values,
-                        func=ACT.Square,
-                        accum_out=sumsq_of[j][:, h : h + 1],
-                    )
+                nc.scalar.activation(
+                    out=squared[:, head_cols(h)],
+                    in_=raw_of[j][:, head_cols(h)],
+                    func=ACT.Square,
+                    accum_out=sumsq_of[j][:, h : h + 1],
+                )
+
+        def vector_squares(j):
+            first = scalar_heads(j)
+            if first == HEADS:
+                return
+            stats = small.tile([P, HEADS, 2, 3], F32)
+            for h in range(first, HEADS):
+                nc.vector.bn_stats(
+                    out=stats[:, h, :, :].rearrange("p g c -> p (g c)"),
+                    in_=raw_of[j][:, head_cols(h)],
+                )
+            mean = stats[:, first:HEADS, :, 1]
+            half = small.tile([P, HEADS, 2], F32)
+            nc.vector.tensor_mul(out=half[:, first:HEADS, :], in0=mean, in1=mean)
+            total = small.tile([P, HEADS, 2], F32)
+            nc.vector.scalar_tensor_tensor(
+                out=total[:, first:HEADS, :],
+                in0=half[:, first:HEADS, :],
+                scalar=float(D_HEAD // 2),
+                in1=stats[:, first:HEADS, :, 2],
+                op0=ALU.mult,
+                op1=ALU.add,
+            )
+            nc.vector.tensor_reduce(
+                out=sumsq_of[j][:, first:HEADS],
+                in_=total[:, first:HEADS, :],
+                axis=AXIS.X,
+                op=ALU.add,
+            )
 
         def inverse(j):
             inv = small.tile([P, HEADS], F32)
@@ -127,7 +146,7 @@ def tile_multiheaddistance_t_kernel(tc, batch_s, batch_ro, out):
             gate_of[j] = gate
 
         def vector_share(j):
-            return HEADS if j == ITEMS - 1 else VECTOR_UNITS
+            return HEADS if j == LAST else VECTOR_UNITS
 
         def vector_units(j):
             unit = unit_pool.tile([P, ROW], BF16)
@@ -164,7 +183,7 @@ def tile_multiheaddistance_t_kernel(tc, batch_s, batch_ro, out):
         def regroup(j):
             grouped = grouped_pool.tile([P, ROW], BF16, align_bytes=64)
             pairs = grouped[:].bitcast(F32).rearrange("p (h r u) -> p h r u", h=HEADS, u=2)
-            scalar_banks = T_BANKS if j >= ITEMS - 2 else int(j % 4 != 3)
+            scalar_banks = T_BANKS if j >= LAST - 1 else int(j % 5 % 2 == 0)
             for b in range(T_BANKS):
                 planes = banks_of[j][b][:].rearrange("p (h u) r -> p h r u", u=2)
                 target = pairs[:, b * HEADS_BANK : (b + 1) * HEADS_BANK]
@@ -174,30 +193,36 @@ def tile_multiheaddistance_t_kernel(tc, batch_s, batch_ro, out):
                     nc.vector.tensor_copy(out=target, in_=planes)
             grouped_of[j] = grouped
 
-        def quantise(j):
+        def quantise(j, pieces=1):
             if j == 0:
                 codes, scales = ro_codes, ro_scales
             else:
                 codes = mx_pool.tile([P, HEADS * P], U32, align_bytes=64)
                 scales = mx_pool.tile([P, HEADS * P], U8, align_bytes=64)
-            nc.vector.quantize_mx(
-                out=codes[:].bitcast(FP8X4), scales=scales[:], in_=grouped_of[j][:]
-            )
+            width = HEADS * P // pieces
+            for first in range(0, HEADS * P, width):
+                words = slice(first, first + width)
+                nc.vector.quantize_mx(
+                    out=codes[:, words].bitcast(FP8X4),
+                    scales=scales[:, words],
+                    in_=grouped_of[j][:, 4 * first : 4 * (first + width)],
+                )
             codes_of[j] = codes
             scales_of[j] = scales
 
         def matmuls(j):
             accs = []
             for a in range(ACC_BANKS):
-                acc = acc_psum.tile([P, HEADS_ACC, P], F32)
-                for i in range(HEADS_ACC):
-                    rows = head_rows(a * HEADS_ACC + i)
+                acc = acc_psum.tile([P, HEADS, RO_ACC], F32)
+                for h in range(HEADS):
+                    rows = head_rows(h)
+                    ro_rows = slice(h * P + a * RO_ACC, h * P + (a + 1) * RO_ACC)
                     nc.tensor.matmul_mx(
-                        out=acc[:, i, :],
+                        out=acc[:, h, :],
                         lhsT=codes_of[j][:, rows].bitcast(FP8X4),
                         lhsT_scale=scales_of[j][:, rows],
-                        rhs=ro_codes[:, rows].bitcast(FP8X4),
-                        rhs_scale=ro_scales[:, rows],
+                        rhs=ro_codes[:, ro_rows].bitcast(FP8X4),
+                        rhs_scale=ro_scales[:, ro_rows],
                         start=True,
                         stop=True,
                     )
@@ -205,30 +230,17 @@ def tile_multiheaddistance_t_kernel(tc, batch_s, batch_ro, out):
             acc_of[j] = accs
 
         def head_max(j):
-            t = j - 1
-            place = t % STORE_TILES
-            if place == 0:
-                part = part_pool.tile([P, STORE_TILES, ACC_BANKS, P], F32)
-                part_of[t // STORE_TILES] = part
-            part = part_of[t // STORE_TILES]
             for a in range(ACC_BANKS):
                 nc.vector.tensor_reduce(
-                    out=part[:, place, a, :],
+                    out=result[:, j - 1, a * RO_ACC : (a + 1) * RO_ACC],
                     in_=acc_of[j][a][:].rearrange("p h m -> p m h"),
                     axis=AXIS.X,
                     op=ALU.max,
                 )
 
-        def join(j):
-            t = j - 1
-            place = t % STORE_TILES
-            part = part_of[t // STORE_TILES]
-            if place == STORE_TILES - 1:
-                done = slice(t - place, t + 1)
-                nc.vector.tensor_max(
-                    out=result[:, done, :], in0=part[:, :, 0, :], in1=part[:, :, 1, :]
-                )
-                nc.sync.dma_start(out=out_tiles[:, done, :], in_=result[:, done, :])
+        def store(first, last):
+            done = slice(first, last + 1)
+            nc.sync.dma_start(out=out_tiles[:, done, :], in_=result[:, done, :])
 
         def staged(stage, j, *rest, first=0):
             if first <= j < ITEMS:
@@ -237,17 +249,36 @@ def tile_multiheaddistance_t_kernel(tc, batch_s, batch_ro, out):
         ctx.enter_context(tc.manual_schedule())
         for j in range(LOADS_AHEAD):
             load(j)
-        for k in range(ITEMS + 4):
+        for k in range(ITEMS):
             staged(load, k + LOADS_AHEAD)
             staged(quantise, k - 3)
             staged(matmuls, k - 3, first=1)
             staged(squares, k, range(1))
+            staged(vector_squares, k)
             staged(inverse, k - 1)
             staged(vector_units, k - 1)
-            staged(join, k - 4, first=1)
             staged(release, k - 1)
             staged(gpsimd_units, k - 1)
             staged(regroup, k - 2)
             staged(transposes, k - 1)
             staged(head_max, k - 3, first=1)
-            staged(squares, k, range(1, HEADS))
+            t = k - 4
+            if t >= 0 and t % STORE_TILES == STORE_TILES - 1:
+                store(t + 1 - STORE_TILES, t)
+            staged(squares, k, range(1, scalar_heads(k)))
+        quantise(LAST - 2)
+        matmuls(LAST - 2)
+        inverse(LAST)
+        vector_units(LAST)
+        transposes(LAST)
+        regroup(LAST - 1)
+        head_max(LAST - 2)
+        quantise(LAST - 1)
+        matmuls(LAST - 1)
+        regroup(LAST)
+        quantise(LAST, pieces=2)
+        head_max(LAST - 1)
+        matmuls(LAST)
+        store(S_TILES - STORE_TILES, S_TILES - 2)
+        head_max(LAST)
+        store(S_TILES - 1, S_TILES - 1)

@@ -29,6 +29,7 @@ ACC_BANKS = P // RO_ACC
 STORE_TILES = 4
 VECTOR_UNITS = 5
 HEAD_SQUARES = (4, 5, 6, 7)
+UNITS_AFTER_RELEASE = 2
 LOAD_PIECES = 4
 LOADS_AHEAD = 2
 
@@ -151,6 +152,8 @@ def tile_multiheaddistance_t_kernel(tc, batch_s, batch_ro, out):
         def vector_units(j):
             unit = unit_pool.tile([P, ROW], BF16)
             for h in range(vector_share(j)):
+                if h == vector_share(j) - UNITS_AFTER_RELEASE and j < LAST:
+                    release(j)
                 nc.vector.tensor_scalar_mul(
                     out=unit[:, head_cols(h)],
                     in0=raw_of[j][:, head_cols(h)],
@@ -257,7 +260,6 @@ def tile_multiheaddistance_t_kernel(tc, batch_s, batch_ro, out):
             staged(vector_squares, k)
             staged(inverse, k - 1)
             staged(vector_units, k - 1)
-            staged(release, k - 1)
             staged(gpsimd_units, k - 1)
             staged(regroup, k - 2)
             staged(transposes, k - 1)

from contextlib import ExitStack

import concourse.mybir as mybir
from concourse.masks import make_identity

F32 = mybir.dt.float32
BF16 = mybir.dt.bfloat16
U32 = mybir.dt.uint32
U8 = mybir.dt.uint8
FP8X4 = mybir.dt.float8_e4m3fn_x4
ACT = mybir.ActivationFunctionType
ALU = mybir.AluOpType
AXIS = mybir.AxisListType

P = 128
HEADS = 8
D_HEAD = 512
ROW = HEADS * D_HEAD
N_ROWS = 4096
S_TILES = N_ROWS // P
LAST = S_TILES
ITEMS = 1 + S_TILES
WORDS_HEAD = D_HEAD // 2
BANK_WORDS = 512
HEADS_BANK = BANK_WORDS // WORDS_HEAD
T_BANKS = HEADS // HEADS_BANK
RO_ACC = BANK_WORDS // HEADS
ACC_BANKS = P // RO_ACC
STORE_TILES = 4
VECTOR_UNITS = 5
HEAD_SQUARES = (4, 5, 6, 7)
UNITS_AFTER_RELEASE = 2
LOAD_PIECES = 4
LOADS_AHEAD = 2

FLOPS = 2 * N_ROWS * P * ROW


def tile_multiheaddistance_t_kernel(tc, batch_s, batch_ro, out):
    nc = tc.nc

    s_tiles = batch_s.rearrange("(p t) d -> p t d", t=S_TILES)
    out_tiles = out.rearrange("(p t) m -> p t m", t=S_TILES)

    with ExitStack() as ctx:
        keep = ctx.enter_context(tc.tile_pool(name="keep", bufs=1))
        raw_pool = ctx.enter_context(tc.tile_pool(name="raw", bufs=LOADS_AHEAD + 2))
        small = ctx.enter_context(tc.tile_pool(name="small", bufs=3))
        unit_pool = ctx.enter_context(tc.tile_pool(name="unit", bufs=2))
        grouped_pool = ctx.enter_context(tc.tile_pool(name="grouped", bufs=2))
        mx_pool = ctx.enter_context(tc.tile_pool(name="mx", bufs=2))
        t_psum = ctx.enter_context(tc.psum_pool(name="t_psum", bufs=T_BANKS + 2))
        acc_psum = ctx.enter_context(tc.psum_pool(name="acc_psum", bufs=ACC_BANKS))

        identity = keep.tile([P, P], F32)
        make_identity(nc, identity[:])

        one = keep.tile([P, 1], F32)
        nc.vector.memset(one[:], 1.0)
        warm = keep.tile([P, 1], F32)
        nc.scalar.activation(out=warm[:], in_=one[:], func=ACT.Abs_reciprocal_sqrt)

        squared = keep.tile([P, ROW], BF16)

        ro_codes = keep.tile([P, HEADS * P], U32, align_bytes=64)
        ro_scales = keep.tile([P, HEADS * P], U8, align_bytes=64)
        result = keep.tile([P, S_TILES, P], F32)

        raw_of = {}
        sumsq_of = {}
        inv_of = {}
        gate_of = {}
        unit_of = {}
        banks_of = {}
        grouped_of = {}
        codes_of = {}
        scales_of = {}
        acc_of = {}

        def head_cols(h):
            return slice(h * D_HEAD, (h + 1) * D_HEAD)

        def head_rows(h):
            return slice(h * P, (h + 1) * P)

        def load(j):
            raw = raw_pool.tile([P, ROW], BF16)
            rows = batch_ro if j == 0 else s_tiles[:, j - 1, :]
            width = ROW // LOAD_PIECES if j < LOADS_AHEAD else ROW
            for first in sorted(range(0, ROW, width), key=lambda col: col % (ROW // 2)):
                cols = slice(first, first + width)
                nc.sync.dma_start(out=raw[:, cols], in_=rows[:, cols])
            raw_of[j] = raw

        def scalar_heads(j):
            return HEAD_SQUARES[j] if j < len(HEAD_SQUARES) else HEADS

        def squares(j, heads):
            if 0 in heads:
                sumsq = small.tile([P, HEADS], F32)
                sumsq_of[j] = sumsq
            for h in heads:
                nc.scalar.activation(
                    out=squared[:, head_cols(h)],
                    in_=raw_of[j][:, head_cols(h)],
                    func=ACT.Square,
                    accum_out=sumsq_of[j][:, h : h + 1],
                )

        def vector_squares(j):
            first = scalar_heads(j)
            if first == HEADS:
                return
            stats = small.tile([P, HEADS, 2, 3], F32)
            for h in range(first, HEADS):
                nc.vector.bn_stats(
                    out=stats[:, h, :, :].rearrange("p g c -> p (g c)"),
                    in_=raw_of[j][:, head_cols(h)],
                )
            mean = stats[:, first:HEADS, :, 1]
            half = small.tile([P, HEADS, 2], F32)
            nc.vector.tensor_mul(out=half[:, first:HEADS, :], in0=mean, in1=mean)
            total = small.tile([P, HEADS, 2], F32)
            nc.vector.scalar_tensor_tensor(
                out=total[:, first:HEADS, :],
                in0=half[:, first:HEADS, :],
                scalar=float(D_HEAD // 2),
                in1=stats[:, first:HEADS, :, 2],
                op0=ALU.mult,
                op1=ALU.add,
            )
            nc.vector.tensor_reduce(
                out=sumsq_of[j][:, first:HEADS],
                in_=total[:, first:HEADS, :],
                axis=AXIS.X,
                op=ALU.add,
            )

        def inverse(j):
            inv = small.tile([P, HEADS], F32)
            nc.scalar.activation(out=inv[:], in_=sumsq_of[j][:], func=ACT.Abs_reciprocal_sqrt)
            inv_of[j] = inv

        def release(j):
            gate = small.tile([P, HEADS], F32)
            nc.vector.tensor_copy(out=gate[:], in_=inv_of[j][:])
            gate_of[j] = gate

        def vector_share(j):
            return HEADS if j == LAST else VECTOR_UNITS

        def vector_units(j):
            unit = unit_pool.tile([P, ROW], BF16)
            for h in range(vector_share(j)):
                if h == vector_share(j) - UNITS_AFTER_RELEASE and j < LAST:
                    release(j)
                nc.vector.tensor_scalar_mul(
                    out=unit[:, head_cols(h)],
                    in0=raw_of[j][:, head_cols(h)],
                    scalar1=inv_of[j][:, h : h + 1],
                )
            unit_of[j] = unit

        def gpsimd_units(j):
            for h in range(vector_share(j), HEADS):
                nc.gpsimd.tensor_scalar(
                    out=unit_of[j][:, head_cols(h)],
                    in0=raw_of[j][:, head_cols(h)],
                    scalar1=gate_of[j][:, h : h + 1],
                    scalar2=0.0,
                    op0=ALU.mult,
                    op1=ALU.add,
                )

        def transposes(j):
            words = unit_of[j][:].bitcast(F32)
            banks = []
            for b in range(T_BANKS):
                bank = t_psum.tile([P, 2 * HEADS_BANK, P], F32)
                for plane in range(2 * HEADS_BANK):
                    first = (b * 2 * HEADS_BANK + plane) * P
                    nc.tensor.transpose(bank[:, plane, :], words[:, first : first + P], identity[:])
                banks.append(bank)
            banks_of[j] = banks

        def regroup(j):
            grouped = grouped_pool.tile([P, ROW], BF16, align_bytes=64)
            pairs = grouped[:].bitcast(F32).rearrange("p (h r u) -> p h r u", h=HEADS, u=2)
            scalar_banks = T_BANKS if j >= LAST - 1 else int(j % 5 % 2 == 0)
            for b in range(T_BANKS):
                planes = banks_of[j][b][:].rearrange("p (h u) r -> p h r u", u=2)
                target = pairs[:, b * HEADS_BANK : (b + 1) * HEADS_BANK]
                if b < scalar_banks:
                    nc.scalar.copy(out=target, in_=planes)
                else:
                    nc.vector.tensor_copy(out=target, in_=planes)
            grouped_of[j] = grouped

        def quantise(j, pieces=1):
            if j == 0:
                codes, scales = ro_codes, ro_scales
            else:
                codes = mx_pool.tile([P, HEADS * P], U32, align_bytes=64)
                scales = mx_pool.tile([P, HEADS * P], U8, align_bytes=64)
            width = HEADS * P // pieces
            for first in range(0, HEADS * P, width):
                words = slice(first, first + width)
                nc.vector.quantize_mx(
                    out=codes[:, words].bitcast(FP8X4),
                    scales=scales[:, words],
                    in_=grouped_of[j][:, 4 * first : 4 * (first + width)],
                )
            codes_of[j] = codes
            scales_of[j] = scales

        def matmuls(j):
            accs = []
            for a in range(ACC_BANKS):
                acc = acc_psum.tile([P, HEADS, RO_ACC], F32)
                for h in range(HEADS):
                    rows = head_rows(h)
                    ro_rows = slice(h * P + a * RO_ACC, h * P + (a + 1) * RO_ACC)
                    nc.tensor.matmul_mx(
                        out=acc[:, h, :],
                        lhsT=codes_of[j][:, rows].bitcast(FP8X4),
                        lhsT_scale=scales_of[j][:, rows],
                        rhs=ro_codes[:, ro_rows].bitcast(FP8X4),
                        rhs_scale=ro_scales[:, ro_rows],
                        start=True,
                        stop=True,
                    )
                accs.append(acc)
            acc_of[j] = accs

        def head_max(j):
            for a in range(ACC_BANKS):
                nc.vector.tensor_reduce(
                    out=result[:, j - 1, a * RO_ACC : (a + 1) * RO_ACC],
                    in_=acc_of[j][a][:].rearrange("p h m -> p m h"),
                    axis=AXIS.X,
                    op=ALU.max,
                )

        def store(first, last):
            done = slice(first, last + 1)
            nc.sync.dma_start(out=out_tiles[:, done, :], in_=result[:, done, :])

        def staged(stage, j, *rest, first=0):
            if first <= j < ITEMS:
                stage(j, *rest)

        ctx.enter_context(tc.manual_schedule())
        for j in range(LOADS_AHEAD):
            load(j)
        for k in range(ITEMS):
            staged(load, k + LOADS_AHEAD)
            staged(quantise, k - 3)
            staged(matmuls, k - 3, first=1)
            staged(squares, k, range(1))
            staged(vector_squares, k)
            staged(inverse, k - 1)
            staged(vector_units, k - 1)
            staged(gpsimd_units, k - 1)
            staged(regroup, k - 2)
            staged(transposes, k - 1)
            staged(head_max, k - 3, first=1)
            t = k - 4
            if t >= 0 and t % STORE_TILES == STORE_TILES - 1:
                store(t + 1 - STORE_TILES, t)
            staged(squares, k, range(1, scalar_heads(k)))
        quantise(LAST - 2)
        matmuls(LAST - 2)
        inverse(LAST)
        vector_units(LAST)
        transposes(LAST)
        regroup(LAST - 1)
        head_max(LAST - 2)
        quantise(LAST - 1)
        matmuls(LAST - 1)
        regroup(LAST)
        quantise(LAST, pieces=2)
        head_max(LAST - 1)
        matmuls(LAST)
        store(S_TILES - STORE_TILES, S_TILES - 2)
        head_max(LAST)
        store(S_TILES - 1, S_TILES - 1)
